import numpy as np
import ml_dtypes


def mxq(x, axis, fmt="e4m3"):
    dtype, down = {"e4m3": (ml_dtypes.float8_e4m3fn, 7), "e5m2": (ml_dtypes.float8_e5m2, 14)}[fmt]
    v = np.moveaxis(np.asarray(x, np.float32).astype(ml_dtypes.bfloat16).astype(np.float64), axis, -1)
    blocks = v.reshape(v.shape[:-1] + (-1, 32))
    amax = np.abs(blocks).max(-1, keepdims=True)
    byte = np.maximum(np.where(amax > 0, np.frexp(amax)[1] - 1 + 127, 0) - down, 1)
    scale = np.exp2(byte - 127.0)
    codes = (blocks / scale).astype(np.float32).astype(dtype).astype(np.float64)
    return np.moveaxis((codes * scale).reshape(v.shape), -1, axis)


WIDE = False


def mx_kscale(k):
    if not WIDE:
        return np.ones(k)
    levels = np.array([10, -10, 5, -5, 0])
    if k % 512:
        return np.exp2(np.random.permutation(np.resize(levels, k // 32))).repeat(32)
    a = np.empty((k // 512, 16))
    for p in range(k // 512):
        a[p, :8] = np.random.permutation(np.resize(levels, 8))
        for g in range(8):
            far = levels[np.abs(levels - a[p, g]) >= 10]
            a[p, g + 8] = far[np.random.randint(len(far))]
    return np.exp2(a.ravel()).repeat(32)


BF16 = ml_dtypes.bfloat16


def bf(x):
    return np.asarray(x, np.float32).astype(BF16)


def f64(x):
    return np.asarray(x).astype(np.float64)


B, T, D, A, H, E = 4, 512, 1024, 1024, 4, 2048
DH = A // H
EPS = 1e-5


def layernorm(v, w, b):
    mu = v.mean(-1, keepdims=True)
    var = np.square(v - mu).mean(-1, keepdims=True)
    return (v - mu) / np.sqrt(var + EPS) * w + b


def setup_inputs():
    s = mx_kscale(D)
    return {'x': bf(np.random.standard_normal((B, T, D))),
            'ln_w': bf((1.0 + 0.1 * np.random.standard_normal(D)) * s),
            'ln_b': bf(0.1 * np.random.standard_normal(D) * s),
            'q_w': bf(np.random.standard_normal((D, A)) * 1.5 / np.sqrt(D) / s[:, None]),
            'q_b': bf(np.random.standard_normal(A) * 0.3)}


def reference(x, ln_w, ln_b, q_w, q_b):
    xn = layernorm(f64(x), f64(ln_w), f64(ln_b))
    q = (mxq(xn, 2, 'e4m3') @ mxq(f64(q_w), 0, 'e4m3')) + f64(q_b)
    q = q.reshape(B, T, H, DH)
    e = np.exp(q - q.max(-1, keepdims=True))
    return (e / e.sum(-1, keepdims=True)).reshape(B, T, A)

@@ -1,0 +1,312 @@
+from contextlib import ExitStack
+
+import concourse.mybir as mybir
+from concourse.masks import make_identity
+
+F32 = mybir.dt.float32
+BF16 = mybir.dt.bfloat16
+U32 = mybir.dt.uint32
+U8 = mybir.dt.uint8
+FP8X4 = mybir.dt.float8_e4m3fn_x4
+ALU = mybir.AluOpType
+ACT = mybir.ActivationFunctionType
+AXIS = mybir.AxisListType
+
+P = 128
+TOKENS = 4 * 512
+D = 1024
+A = 1024
+HEADS = 4
+HEAD_COLS = A // HEADS
+EPS = 1e-5
+
+PACK = 4
+K_PASS = P * PACK
+PASSES = D // K_PASS
+CHUNKS = D // P
+TILES = TOKENS // P
+SUBTILES = 2
+BLOCK = P * SUBTILES
+BLOCKS = TOKENS // BLOCK
+BANK = 512
+HALVES = A // BANK
+STAT_COLS = 512
+STAT_DIM = 6
+
+assert SUBTILES == PASSES
+LEAD_STATS = 10
+LEAD_MOMENTS = 9
+LEAD_CENTRE = 8
+LEAD_TRANSPOSE = 5
+LEAD_QUANTISE = 3
+LEAD_MATMUL = 2
+LEAD_BIAS = 1
+LAG_EXP = 1
+LAG_SCALE = 2
+WEIGHTS_STEP = -4
+
+FLOPS = 2 * TOKENS * D * A
+
+
+def tile_efficientcrossattention_pa_kernel(tc, x, ln_w, ln_b, q_w, q_b, out):
+    nc = tc.nc
+    x_blocks = x.flatten_outer_dims().rearrange("(b p i) k -> b p i k", p=P, i=SUBTILES)
+    out_blocks = out.flatten_outer_dims().rearrange("(b p i) a -> b p i a", p=P, i=SUBTILES)
+
+    with ExitStack() as ctx:
+        const = ctx.enter_context(tc.tile_pool(name="const", bufs=1))
+        x_pool = ctx.enter_context(tc.tile_pool(name="x", bufs=BLOCKS))
+        hat_pool = ctx.enter_context(tc.tile_pool(name="hat", bufs=6))
+        norm_pool = ctx.enter_context(tc.tile_pool(name="norm", bufs=4))
+        code_pool = ctx.enter_context(tc.tile_pool(name="code", bufs=6))
+        small = ctx.enter_context(tc.tile_pool(name="small", bufs=16))
+        soft_pool = ctx.enter_context(tc.tile_pool(name="soft", bufs=4))
+        psum_t = ctx.enter_context(tc.psum_pool(name="psum_t", bufs=4))
+        psum_q = ctx.enter_context(tc.psum_pool(name="psum_q", bufs=4))
+        ctx.enter_context(tc.manual_schedule())
+
+        affine_bf = const.tile([P, 2, 2, PASSES, PACK], BF16)
+        for s, vec in enumerate((ln_w, ln_b)):
+            nc.sync.dma_start(out=affine_bf[:, s, 0], in_=vec.rearrange("(g p j) -> p g j", p=P, j=PACK))
+        x_tiles = []
+        for b in range(BLOCKS):
+            x_blk = x_pool.tile([P, SUBTILES, D], BF16)
+            x_tiles.append(x_blk)
+        for b in range(2):
+            nc.sync.dma_start(out=x_tiles[b][:], in_=x_blocks[b])
+        bias_bc = const.tile([P, A], BF16)
+        nc.sync.dma_start(out=bias_bc[:], in_=q_b.partition_broadcast(P))
+        w_raw = const.tile([P, PASSES, PACK, A], BF16)
+        w_view = q_w.rearrange("(g p j) n -> g p j n", j=PACK, p=P)
+        for g in range(PASSES):
+            nc.sync.dma_start(out=w_raw[:, g], in_=w_view[g])
+        for b in range(2, BLOCKS):
+            nc.sync.dma_start(out=x_tiles[b][:], in_=x_blocks[b])
+
+        ident = const.tile([P, P], F32)
+        make_identity(nc, ident[:])
+        neg_half = const.tile([P, SUBTILES], F32)
+        nc.vector.memset(neg_half[:], -0.5)
+        affine = const.tile([P, 2 * CHUNKS], F32)
+        nc.vector.tensor_copy(
+            out=affine[:].rearrange("p (s c) -> p s c", s=2),
+            in_=affine_bf[:, :, 0].rearrange("p s g j -> p s (g j)"),
+        )
+
+        w_grouped = const.tile([P, PASSES, A, PACK], BF16, align_bytes=64)
+        w_codes = const.tile([P, PASSES, A], U32, align_bytes=64)
+        w_scales = const.tile([P, PASSES, A], U8, align_bytes=64)
+
+        def regroup_weights(copy, g):
+            for n in range(HALVES):
+                cols = slice(n * BANK, (n + 1) * BANK)
+                copy(
+                    out=w_grouped[:, g, cols, :].rearrange("p (c i) j -> p c j i", i=4),
+                    in_=w_raw[:, g, :, cols].rearrange("p j (c i) -> p c j i", i=4),
+                )
+
+        def quantise_weights():
+            for g in range(PASSES):
+                for n in range(HALVES):
+                    cols = slice(n * BANK, (n + 1) * BANK)
+                    nc.vector.quantize_mx(
+                        out=w_codes[:, g, cols].bitcast(FP8X4),
+                        scales=w_scales[:, g, cols],
+                        in_=w_grouped[:, g, cols, :].rearrange("p n j -> p (n j)"),
+                    )
+
+        stat_tiles = {}
+        mean_vars = {}
+        moments = {}
+        x_hats = {}
+        plane_tiles = {}
+        grouped_tiles = {}
+        operands = {}
+        accs = {}
+        logit_tiles = {}
+        neg_maxes = {}
+        expo_tiles = {}
+        inverse_sums = {}
+        prob_tiles = {}
+
+        def partial_stats(t):
+            stat = small.tile([P, (D // STAT_COLS) * STAT_DIM], F32)
+            for h in range(D // STAT_COLS):
+                nc.vector.bn_stats(
+                    out=stat[:, h * STAT_DIM : (h + 1) * STAT_DIM],
+                    in_=x_tiles[t // SUBTILES][:, t % SUBTILES, h * STAT_COLS : (h + 1) * STAT_COLS],
+                )
+            stat_tiles[t] = stat
+
+        def aggregate(t):
+            if t % SUBTILES == 0:
+                mean_var = small.tile([P, SUBTILES, 2], F32)
+                mean_vars[t // SUBTILES] = mean_var
+            nc.vector.bn_aggr(out=mean_vars[t // SUBTILES][:, t % SUBTILES, :], in_=stat_tiles[t][:])
+
+        def finish_moments(t):
+            if t % SUBTILES == SUBTILES - 1:
+                mean_var = mean_vars[t // SUBTILES]
+                neg_mean = small.tile([P, SUBTILES], F32)
+                nc.vector.tensor_scalar_mul(out=neg_mean[:], in0=mean_var[:, :, 0], scalar1=-1.0)
+                var_eps = small.tile([P, SUBTILES], F32)
+                nc.vector.tensor_scalar_add(out=var_eps[:], in0=mean_var[:, :, 1], scalar1=EPS)
+                rstd = small.tile([P, SUBTILES], F32)
+                nc.gpsimd.tensor_tensor(out=rstd[:], in0=var_eps[:], in1=neg_half[:], op=ALU.pow)
+                moments[t // SUBTILES] = (neg_mean, rstd)
+
+        def centre(t):
+            neg_mean, rstd = moments[t // SUBTILES]
+            i = t % SUBTILES
+            x_hat = hat_pool.tile([P, D], F32)
+            engine = nc.gpsimd if t % 2 == 0 else nc.vector
+            engine.tensor_scalar(
+                out=x_hat[:].rearrange("q (g j p) -> q g j p", g=PASSES, j=PACK),
+                in0=x_tiles[t // SUBTILES][:, i, :].rearrange("q (g p j) -> q g j p", g=PASSES, j=PACK),
+                scalar1=neg_mean[:, i : i + 1],
+                scalar2=rstd[:, i : i + 1],
+                op0=ALU.add,
+                op1=ALU.mult,
+            )
+            x_hats[t] = x_hat
+
+        def transpose_affine(v):
+            b, g = v // PASSES, v % PASSES
+            planes = norm_pool.tile([P, PACK, BLOCK], BF16)
+            for j in range(PACK):
+                c = g * PACK + j
+                bank = psum_t.tile([P, BANK], F32, tag="bank")
+                for i in range(SUBTILES):
+                    nc.tensor.transpose(
+                        bank[:, i * P : (i + 1) * P], x_hats[b * SUBTILES + i][:, c * P : (c + 1) * P], ident[:]
+                    )
+                nc.scalar.activation(
+                    out=planes[:, j, :],
+                    in_=bank[:, 0:BLOCK],
+                    func=ACT.Identity,
+                    scale=affine[:, c : c + 1],
+                    bias=affine[:, CHUNKS + c : CHUNKS + c + 1],
+                )
+            plane_tiles[v] = planes
+
+        def regroup(v):
+            grouped = norm_pool.tile([P, BLOCK, PACK], BF16, align_bytes=64)
+            nc.scalar.copy(
+                out=grouped[:].rearrange("p (c i) j -> p c j i", i=4),
+                in_=plane_tiles[v][:].rearrange("p j (c i) -> p c j i", i=4),
+            )
+            grouped_tiles[v] = grouped
+
+        def quantise(v):
+            x_codes = code_pool.tile([P, BLOCK], U32, align_bytes=64)
+            x_scales = code_pool.tile([P, BLOCK], U8, align_bytes=64)
+            nc.vector.quantize_mx(
+                out=x_codes[:].bitcast(FP8X4),
+                scales=x_scales[:],
+                in_=grouped_tiles[v][:].rearrange("p t j -> p (t j)"),
+            )
+            operands[v] = (x_codes, x_scales)
+
+        def matmuls(t):
+            b, i = t // SUBTILES, t % SUBTILES
+            tok = slice(i * P, (i + 1) * P)
+            for n in range(HALVES):
+                cols = slice(n * BANK, (n + 1) * BANK)
+                acc = psum_q.tile([P, BANK], F32)
+                for g in range(PASSES):
+                    x_codes, x_scales = operands[b * PASSES + g]
+                    nc.tensor.matmul_mx(
+                        out=acc[:],
+                        lhsT=x_codes[:, tok].bitcast(FP8X4),
+                        lhsT_scale=x_scales[:, tok],
+                        rhs=w_codes[:, g, cols].bitcast(FP8X4),
+                        rhs_scale=w_scales[:, g, cols],
+                        start=(g == 0),
+                        stop=(g == PASSES - 1),
+                    )
+                accs[(t, n)] = acc
+
+        def add_bias(t):
+            logits = soft_pool.tile([P, A], F32)
+            for n in range(HALVES):
+                cols = slice(n * BANK, (n + 1) * BANK)
+                nc.vector.tensor_tensor(out=logits[:, cols], in0=accs[(t, n)][:], in1=bias_bc[:, cols], op=ALU.add)
+            logit_tiles[t] = logits
+
+        def row_max(t):
+            neg_max = small.tile([P, HEADS], F32)
+            nc.vector.tensor_reduce(
+                out=neg_max[:],
+                in_=logit_tiles[t][:].rearrange("p (h d) -> p h d", h=HEADS),
+                axis=AXIS.X,
+                op=ALU.max,
+                negate=True,
+            )
+            neg_maxes[t] = neg_max
+
+        def exponentials(t):
+            expo = soft_pool.tile([P, A], F32)
+            sums = small.tile([P, HEADS], F32)
+            for h in range(HEADS):
+                head = slice(h * HEAD_COLS, (h + 1) * HEAD_COLS)
+                nc.scalar.activation(
+                    out=expo[:, head],
+                    in_=logit_tiles[t][:, head],
+                    func=ACT.Exp,
+                    bias=neg_maxes[t][:, h : h + 1],
+                    scale=1.0,
+                    accum_out=sums[:, h : h + 1],
+                )
+            expo_tiles[t] = (expo, sums)
+
+        def invert_sums(t):
+            inv_sums = small.tile([P, HEADS], F32)
+            nc.vector.reciprocal(out=inv_sums[:], in_=expo_tiles[t][1][:])
+            inverse_sums[t] = inv_sums
+
+        def scale_on_vector(t):
+            probs = soft_pool.tile([P, A], F32)
+            for h in range(HEADS // 2):
+                head = slice(h * HEAD_COLS, (h + 1) * HEAD_COLS)
+                nc.vector.tensor_scalar_mul(
+                    out=probs[:, head],
+                    in0=expo_tiles[t][0][:, head],
+                    scalar1=inverse_sums[t][:, h : h + 1],
+                )
+            prob_tiles[t] = probs
+
+        def scale_on_scalar_store(t):
+            probs = prob_tiles[t]
+            for h in range(HEADS // 2, HEADS):
+                head = slice(h * HEAD_COLS, (h + 1) * HEAD_COLS)
+                nc.scalar.activation(
+                    out=probs[:, head],
+                    in_=expo_tiles[t][0][:, head],
+                    func=ACT.Copy,
+                    scale=inverse_sums[t][:, h : h + 1],
+                )
+            nc.sync.dma_start(out=out_blocks[t // SUBTILES][:, t % SUBTILES, :], in_=probs[:])
+
+        def run(stage, index):
+            if 0 <= index < TILES:
+                stage(index)
+
+        regroup_weights(nc.scalar.copy, 0)
+        for step in range(-LEAD_STATS, TILES + LAG_SCALE):
+            if step == WEIGHTS_STEP:
+                regroup_weights(nc.vector.tensor_copy, 1)
+                quantise_weights()
+            run(quantise, step + LEAD_QUANTISE)
+            run(invert_sums, step - LAG_SCALE)
+            run(add_bias, step + LEAD_BIAS)
+            run(scale_on_vector, step - LAG_SCALE)
+            run(aggregate, step + LEAD_MOMENTS)
+            run(row_max, step)
+            run(partial_stats, step + LEAD_STATS)
+            run(finish_moments, step + LEAD_MOMENTS)
+            run(transpose_affine, step + LEAD_TRANSPOSE)
+            run(matmuls, step + LEAD_MATMUL)
+            run(exponentials, step - LAG_EXP)
+            run(scale_on_scalar_store, step - LAG_SCALE)
+            run(regroup, step + LEAD_TRANSPOSE)
+            run(centre, step + LEAD_CENTRE)

@@ -67,15 +67,16 @@ def tile_efficientcrossattention_pa_kernel(tc, x, ln_w, ln_b, q_w, q_b, out):
 
         affine_bf = const.tile([P, 2, 2, PASSES, PACK], BF16)
         for s, vec in enumerate((ln_w, ln_b)):
-            nc.sync.dma_start(out=affine_bf[:, s, 0], in_=vec.rearrange("(g p j) -> p g j", p=P, j=PACK))
+            nc.scalar.dma_start(out=affine_bf[:, s, 0], in_=vec.rearrange("(g p j) -> p g j", p=P, j=PACK))
+        bias_row = const.tile([P, A], BF16)
+        nc.vector.memset(bias_row[:], 0.0)
+        nc.scalar.dma_start(out=bias_row[0:1, :], in_=q_b.unsqueeze(0))
         x_tiles = []
         for b in range(BLOCKS):
             x_blk = x_pool.tile([P, SUBTILES, D], BF16)
             x_tiles.append(x_blk)
         for b in range(2):
             nc.sync.dma_start(out=x_tiles[b][:], in_=x_blocks[b])
-        bias_bc = const.tile([P, A], BF16)
-        nc.sync.dma_start(out=bias_bc[:], in_=q_b.partition_broadcast(P))
         w_raw = const.tile([P, PASSES, PACK, A], BF16)
         w_view = q_w.rearrange("(g p j) n -> g p j n", j=PACK, p=P)
         for g in range(PASSES):
@@ -92,6 +93,15 @@ def tile_efficientcrossattention_pa_kernel(tc, x, ln_w, ln_b, q_w, q_b, out):
             out=affine[:].rearrange("p (s c) -> p s c", s=2),
             in_=affine_bf[:, :, 0].rearrange("p s g j -> p s (g j)"),
         )
+
+        ones = const.tile([P, P], BF16)
+        nc.vector.memset(ones[:], 1.0)
+        bias_bc = const.tile([P, A], BF16)
+        for n in range(HALVES):
+            cols = slice(n * BANK, (n + 1) * BANK)
+            bias_bank = psum_q.tile([P, BANK], F32, tag="acc")
+            nc.tensor.matmul(bias_bank[:], lhsT=ones[:], rhs=bias_row[:, cols], start=True, stop=True)
+            nc.scalar.copy(out=bias_bc[:, cols], in_=bias_bank[:])
 
         w_grouped = const.tile([P, PASSES, A, PACK], BF16, align_bytes=64)
         w_codes = const.tile([P, PASSES, A], U32, align_bytes=64)
@@ -212,7 +222,7 @@ def tile_efficientcrossattention_pa_kernel(tc, x, ln_w, ln_b, q_w, q_b, out):
             tok = slice(i * P, (i + 1) * P)
             for n in range(HALVES):
                 cols = slice(n * BANK, (n + 1) * BANK)
-                acc = psum_q.tile([P, BANK], F32)
+                acc = psum_q.tile([P, BANK], F32, tag="acc")
                 for g in range(PASSES):
                     x_codes, x_scales = operands[b * PASSES + g]
                     nc.tensor.matmul_mx(

@@ -43,7 +43,6 @@ LEAD_MATMUL = 2
 LEAD_BIAS = 1
 LAG_EXP = 1
 LAG_SCALE = 2
-WEIGHTS_STEP = -4
 
 FLOPS = 2 * TOKENS * D * A
 
@@ -56,11 +55,11 @@ def tile_efficientcrossattention_pa_kernel(tc, x, ln_w, ln_b, q_w, q_b, out):
     with ExitStack() as ctx:
         const = ctx.enter_context(tc.tile_pool(name="const", bufs=1))
         x_pool = ctx.enter_context(tc.tile_pool(name="x", bufs=BLOCKS))
-        hat_pool = ctx.enter_context(tc.tile_pool(name="hat", bufs=6))
-        norm_pool = ctx.enter_context(tc.tile_pool(name="norm", bufs=4))
+        hat_pool = ctx.enter_context(tc.tile_pool(name="hat", bufs=8))
+        norm_pool = ctx.enter_context(tc.tile_pool(name="norm", bufs=6))
         code_pool = ctx.enter_context(tc.tile_pool(name="code", bufs=6))
         small = ctx.enter_context(tc.tile_pool(name="small", bufs=16))
-        soft_pool = ctx.enter_context(tc.tile_pool(name="soft", bufs=4))
+        soft_pool = ctx.enter_context(tc.tile_pool(name="soft", bufs=5))
         psum_t = ctx.enter_context(tc.psum_pool(name="psum_t", bufs=4))
         psum_q = ctx.enter_context(tc.psum_pool(name="psum_q", bufs=4))
         ctx.enter_context(tc.manual_schedule())
@@ -69,39 +68,42 @@ def tile_efficientcrossattention_pa_kernel(tc, x, ln_w, ln_b, q_w, q_b, out):
         for s, vec in enumerate((ln_w, ln_b)):
             nc.scalar.dma_start(out=affine_bf[:, s, 0], in_=vec.rearrange("(g p j) -> p g j", p=P, j=PACK))
         bias_row = const.tile([P, A], BF16)
-        nc.vector.memset(bias_row[:], 0.0)
-        nc.scalar.dma_start(out=bias_row[0:1, :], in_=q_b.unsqueeze(0))
+        nc.gpsimd.memset(bias_row[:], 0.0)
         x_tiles = []
         for b in range(BLOCKS):
             x_blk = x_pool.tile([P, SUBTILES, D], BF16)
             x_tiles.append(x_blk)
-        for b in range(2):
-            nc.sync.dma_start(out=x_tiles[b][:], in_=x_blocks[b])
         w_raw = const.tile([P, PASSES, PACK, A], BF16)
         w_view = q_w.rearrange("(g p j) n -> g p j n", j=PACK, p=P)
-        for g in range(PASSES):
-            nc.sync.dma_start(out=w_raw[:, g], in_=w_view[g])
-        for b in range(2, BLOCKS):
+
+        def load_x(b):
             nc.sync.dma_start(out=x_tiles[b][:], in_=x_blocks[b])
+
+        def load_w(g):
+            nc.sync.dma_start(out=w_raw[:, g], in_=w_view[g])
+
+        load_x(0)
+        load_x(1)
+        load_w(0)
+        load_x(2)
+        nc.sync.dma_start(out=bias_row[0:1, :], in_=q_b.unsqueeze(0))
+        load_w(1)
+        for b in range(3, BLOCKS):
+            load_x(b)
 
         ident = const.tile([P, P], F32)
         make_identity(nc, ident[:])
         neg_half = const.tile([P, SUBTILES], F32)
         nc.vector.memset(neg_half[:], -0.5)
         affine = const.tile([P, 2 * CHUNKS], F32)
-        nc.vector.tensor_copy(
+        nc.scalar.copy(
             out=affine[:].rearrange("p (s c) -> p s c", s=2),
             in_=affine_bf[:, :, 0].rearrange("p s g j -> p s (g j)"),
         )
 
         ones = const.tile([P, P], BF16)
-        nc.vector.memset(ones[:], 1.0)
+        nc.gpsimd.memset(ones[:], 1.0)
         bias_bc = const.tile([P, A], BF16)
-        for n in range(HALVES):
-            cols = slice(n * BANK, (n + 1) * BANK)
-            bias_bank = psum_q.tile([P, BANK], F32, tag="acc")
-            nc.tensor.matmul(bias_bank[:], lhsT=ones[:], rhs=bias_row[:, cols], start=True, stop=True)
-            nc.scalar.copy(out=bias_bc[:, cols], in_=bias_bank[:])
 
         w_grouped = const.tile([P, PASSES, A, PACK], BF16, align_bytes=64)
         w_codes = const.tile([P, PASSES, A], U32, align_bytes=64)
@@ -115,15 +117,14 @@ def tile_efficientcrossattention_pa_kernel(tc, x, ln_w, ln_b, q_w, q_b, out):
                     in_=w_raw[:, g, :, cols].rearrange("p j (c i) -> p c j i", i=4),
                 )
 
-        def quantise_weights():
-            for g in range(PASSES):
-                for n in range(HALVES):
-                    cols = slice(n * BANK, (n + 1) * BANK)
-                    nc.vector.quantize_mx(
-                        out=w_codes[:, g, cols].bitcast(FP8X4),
-                        scales=w_scales[:, g, cols],
-                        in_=w_grouped[:, g, cols, :].rearrange("p n j -> p (n j)"),
-                    )
+        def quantise_weights(g):
+            for n in range(HALVES):
+                cols = slice(n * BANK, (n + 1) * BANK)
+                nc.vector.quantize_mx(
+                    out=w_codes[:, g, cols].bitcast(FP8X4),
+                    scales=w_scales[:, g, cols],
+                    in_=w_grouped[:, g, cols, :].rearrange("p n j -> p (n j)"),
+                )
 
         stat_tiles = {}
         mean_vars = {}
@@ -137,7 +138,6 @@ def tile_efficientcrossattention_pa_kernel(tc, x, ln_w, ln_b, q_w, q_b, out):
         neg_maxes = {}
         expo_tiles = {}
         inverse_sums = {}
-        prob_tiles = {}
 
         def partial_stats(t):
             stat = small.tile([P, (D // STAT_COLS) * STAT_DIM], F32)
@@ -158,9 +158,13 @@ def tile_efficientcrossattention_pa_kernel(tc, x, ln_w, ln_b, q_w, q_b, out):
             if t % SUBTILES == SUBTILES - 1:
                 mean_var = mean_vars[t // SUBTILES]
                 neg_mean = small.tile([P, SUBTILES], F32)
-                nc.vector.tensor_scalar_mul(out=neg_mean[:], in0=mean_var[:, :, 0], scalar1=-1.0)
                 var_eps = small.tile([P, SUBTILES], F32)
-                nc.vector.tensor_scalar_add(out=var_eps[:], in0=mean_var[:, :, 1], scalar1=EPS)
+                nc.gpsimd.tensor_scalar(
+                    out=neg_mean[:], in0=mean_var[:, :, 0], scalar1=-1.0, scalar2=0.0, op0=ALU.mult, op1=ALU.add
+                )
+                nc.gpsimd.tensor_scalar(
+                    out=var_eps[:], in0=mean_var[:, :, 1], scalar1=EPS, scalar2=1.0, op0=ALU.add, op1=ALU.mult
+                )
                 rstd = small.tile([P, SUBTILES], F32)
                 nc.gpsimd.tensor_tensor(out=rstd[:], in0=var_eps[:], in1=neg_half[:], op=ALU.pow)
                 moments[t // SUBTILES] = (neg_mean, rstd)
@@ -169,7 +173,7 @@ def tile_efficientcrossattention_pa_kernel(tc, x, ln_w, ln_b, q_w, q_b, out):
             neg_mean, rstd = moments[t // SUBTILES]
             i = t % SUBTILES
             x_hat = hat_pool.tile([P, D], F32)
-            engine = nc.gpsimd if t % 2 == 0 else nc.vector
+            engine = nc.gpsimd if t >= SUBTILES and t % 2 == 0 else nc.vector
             engine.tensor_scalar(
                 out=x_hat[:].rearrange("q (g j p) -> q g j p", g=PASSES, j=PACK),
                 in0=x_tiles[t // SUBTILES][:, i, :].rearrange("q (g p j) -> q g j p", g=PASSES, j=PACK),
@@ -200,22 +204,26 @@ def tile_efficientcrossattention_pa_kernel(tc, x, ln_w, ln_b, q_w, q_b, out):
             plane_tiles[v] = planes
 
         def regroup(v):
-            grouped = norm_pool.tile([P, BLOCK, PACK], BF16, align_bytes=64)
+            b, g = v // PASSES, v % PASSES
+            if g == 0:
+                grouped = norm_pool.tile([P, PASSES, BLOCK, PACK], BF16, align_bytes=64)
+                grouped_tiles[b] = grouped
             nc.scalar.copy(
-                out=grouped[:].rearrange("p (c i) j -> p c j i", i=4),
+                out=grouped_tiles[b][:, g].rearrange("p (c i) j -> p c j i", i=4),
                 in_=plane_tiles[v][:].rearrange("p j (c i) -> p c j i", i=4),
             )
-            grouped_tiles[v] = grouped
 
         def quantise(v):
-            x_codes = code_pool.tile([P, BLOCK], U32, align_bytes=64)
-            x_scales = code_pool.tile([P, BLOCK], U8, align_bytes=64)
-            nc.vector.quantize_mx(
-                out=x_codes[:].bitcast(FP8X4),
-                scales=x_scales[:],
-                in_=grouped_tiles[v][:].rearrange("p t j -> p (t j)"),
-            )
-            operands[v] = (x_codes, x_scales)
+            if v % PASSES == PASSES - 1:
+                b = v // PASSES
+                x_codes = code_pool.tile([P, PASSES, BLOCK], U32, align_bytes=64)
+                x_scales = code_pool.tile([P, PASSES, BLOCK], U8, align_bytes=64)
+                nc.vector.quantize_mx(
+                    out=x_codes[:].rearrange("p g t -> p (g t)").bitcast(FP8X4),
+                    scales=x_scales[:].rearrange("p g t -> p (g t)"),
+                    in_=grouped_tiles[b][:].rearrange("p g t j -> p (g t j)"),
+                )
+                operands[b] = (x_codes, x_scales)
 
         def matmuls(t):
             b, i = t // SUBTILES, t % SUBTILES
@@ -224,11 +232,11 @@ def tile_efficientcrossattention_pa_kernel(tc, x, ln_w, ln_b, q_w, q_b, out):
                 cols = slice(n * BANK, (n + 1) * BANK)
                 acc = psum_q.tile([P, BANK], F32, tag="acc")
                 for g in range(PASSES):
-                    x_codes, x_scales = operands[b * PASSES + g]
+                    x_codes, x_scales = operands[b]
                     nc.tensor.matmul_mx(
                         out=acc[:],
-                        lhsT=x_codes[:, tok].bitcast(FP8X4),
-                        lhsT_scale=x_scales[:, tok],
+                        lhsT=x_codes[:, g, tok].bitcast(FP8X4),
+                        lhsT_scale=x_scales[:, g, tok],
                         rhs=w_codes[:, g, cols].bitcast(FP8X4),
                         rhs_scale=w_scales[:, g, cols],
                         start=(g == 0),
@@ -274,42 +282,54 @@ def tile_efficientcrossattention_pa_kernel(tc, x, ln_w, ln_b, q_w, q_b, out):
             nc.vector.reciprocal(out=inv_sums[:], in_=expo_tiles[t][1][:])
             inverse_sums[t] = inv_sums
 
-        def scale_on_vector(t):
+        def scale_store(t):
             probs = soft_pool.tile([P, A], F32)
-            for h in range(HEADS // 2):
+            for h in range(HEADS):
                 head = slice(h * HEAD_COLS, (h + 1) * HEAD_COLS)
-                nc.vector.tensor_scalar_mul(
-                    out=probs[:, head],
-                    in0=expo_tiles[t][0][:, head],
-                    scalar1=inverse_sums[t][:, h : h + 1],
-                )
-            prob_tiles[t] = probs
-
-        def scale_on_scalar_store(t):
-            probs = prob_tiles[t]
-            for h in range(HEADS // 2, HEADS):
-                head = slice(h * HEAD_COLS, (h + 1) * HEAD_COLS)
-                nc.scalar.activation(
-                    out=probs[:, head],
-                    in_=expo_tiles[t][0][:, head],
-                    func=ACT.Copy,
-                    scale=inverse_sums[t][:, h : h + 1],
-                )
+                who = "V" if t >= TILES - SUBTILES else "G" if h < 3 else "S"
+                if who == "S":
+                    nc.scalar.activation(
+                        out=probs[:, head],
+                        in_=expo_tiles[t][0][:, head],
+                        func=ACT.Copy,
+                        scale=inverse_sums[t][:, h : h + 1],
+                    )
+                else:
+                    engine = nc.vector if who == "V" else nc.gpsimd
+                    engine.tensor_scalar(
+                        out=probs[:, head],
+                        in0=expo_tiles[t][0][:, head],
+                        scalar1=inverse_sums[t][:, h : h + 1],
+                        scalar2=1.0,
+                        op0=ALU.mult,
+                        op1=ALU.mult,
+                    )
             nc.sync.dma_start(out=out_blocks[t // SUBTILES][:, t % SUBTILES, :], in_=probs[:])
 
         def run(stage, index):
             if 0 <= index < TILES:
                 stage(index)
 
+        def copy_bias():
+            for n in range(HALVES):
+                cols = slice(n * BANK, (n + 1) * BANK)
+                bias_bank = psum_q.tile([P, BANK], F32, tag="acc")
+                nc.tensor.matmul(bias_bank[:], lhsT=ones[:], rhs=bias_row[:, cols], start=True, stop=True)
+                nc.scalar.copy(out=bias_bc[:, cols], in_=bias_bank[:])
+
         regroup_weights(nc.scalar.copy, 0)
         for step in range(-LEAD_STATS, TILES + LAG_SCALE):
-            if step == WEIGHTS_STEP:
+            if step == -4:
+                quantise_weights(0)
+            if step == -4:
                 regroup_weights(nc.vector.tensor_copy, 1)
-                quantise_weights()
+            if step == -2:
+                quantise_weights(1)
+            if step == -3:
+                copy_bias()
             run(quantise, step + LEAD_QUANTISE)
             run(invert_sums, step - LAG_SCALE)
             run(add_bias, step + LEAD_BIAS)
-            run(scale_on_vector, step - LAG_SCALE)
             run(aggregate, step + LEAD_MOMENTS)
             run(row_max, step)
             run(partial_stats, step + LEAD_STATS)
@@ -317,6 +337,6 @@ def tile_efficientcrossattention_pa_kernel(tc, x, ln_w, ln_b, q_w, q_b, out):
             run(transpose_affine, step + LEAD_TRANSPOSE)
             run(matmuls, step + LEAD_MATMUL)
             run(exponentials, step - LAG_EXP)
-            run(scale_on_scalar_store, step - LAG_SCALE)
             run(regroup, step + LEAD_TRANSPOSE)
             run(centre, step + LEAD_CENTRE)
+            run(scale_store, step - LAG_SCALE)

@@ -18,6 +18,8 @@ D = 1024
 A = 1024
 HEADS = 4
 HEAD_COLS = A // HEADS
+HALF_HEADS = HEADS // 2
+LAST_STORES = 3
 EPS = 1e-5
 
 PACK = 4
@@ -39,7 +41,7 @@ LEAD_MOMENTS = 9
 LEAD_CENTRE = 8
 LEAD_TRANSPOSE = 5
 LEAD_QUANTISE = 3
-LEAD_MATMUL = 2
+LEAD_MATMUL = 1
 LEAD_BIAS = 1
 LAG_EXP = 1
 LAG_SCALE = 2
@@ -65,8 +67,6 @@ def tile_efficientcrossattention_pa_kernel(tc, x, ln_w, ln_b, q_w, q_b, out):
         ctx.enter_context(tc.manual_schedule())
 
         affine_bf = const.tile([P, 2, 2, PASSES, PACK], BF16)
-        for s, vec in enumerate((ln_w, ln_b)):
-            nc.scalar.dma_start(out=affine_bf[:, s, 0], in_=vec.rearrange("(g p j) -> p g j", p=P, j=PACK))
         bias_row = const.tile([P, A], BF16)
         nc.gpsimd.memset(bias_row[:], 0.0)
         x_tiles = []
@@ -79,13 +79,20 @@ def tile_efficientcrossattention_pa_kernel(tc, x, ln_w, ln_b, q_w, q_b, out):
         def load_x(b):
             nc.sync.dma_start(out=x_tiles[b][:], in_=x_blocks[b])
 
+        def load_tile(t):
+            b, i = t // SUBTILES, t % SUBTILES
+            nc.sync.dma_start(out=x_tiles[b][:, i, :], in_=x_blocks[b][:, i, :])
+
         def load_w(g):
             nc.sync.dma_start(out=w_raw[:, g], in_=w_view[g])
 
-        load_x(0)
+        load_tile(0)
+        load_tile(1)
         load_x(1)
         load_w(0)
         load_x(2)
+        for s, vec in enumerate((ln_w, ln_b)):
+            nc.sync.dma_start(out=affine_bf[:, s, 0], in_=vec.rearrange("(g p j) -> p g j", p=P, j=PACK))
         nc.sync.dma_start(out=bias_row[0:1, :], in_=q_b.unsqueeze(0))
         load_w(1)
         for b in range(3, BLOCKS):
@@ -95,11 +102,9 @@ def tile_efficientcrossattention_pa_kernel(tc, x, ln_w, ln_b, q_w, q_b, out):
         make_identity(nc, ident[:])
         neg_half = const.tile([P, SUBTILES], F32)
         nc.vector.memset(neg_half[:], -0.5)
+        warm = const.tile([P, 1], F32)
+        nc.scalar.activation(out=warm[:], in_=neg_half[:, 0:1], func=ACT.Exp)
         affine = const.tile([P, 2 * CHUNKS], F32)
-        nc.scalar.copy(
-            out=affine[:].rearrange("p (s c) -> p s c", s=2),
-            in_=affine_bf[:, :, 0].rearrange("p s g j -> p s (g j)"),
-        )
 
         ones = const.tile([P, P], BF16)
         nc.gpsimd.memset(ones[:], 1.0)
@@ -138,6 +143,8 @@ def tile_efficientcrossattention_pa_kernel(tc, x, ln_w, ln_b, q_w, q_b, out):
         neg_maxes = {}
         expo_tiles = {}
         inverse_sums = {}
+        two_halves = [slice(0, HALF_HEADS), slice(HALF_HEADS, HEADS)]
+        prob_tiles = {}
 
         def partial_stats(t):
             stat = small.tile([P, (D // STAT_COLS) * STAT_DIM], F32)
@@ -244,23 +251,40 @@ def tile_efficientcrossattention_pa_kernel(tc, x, ln_w, ln_b, q_w, q_b, out):
                     )
                 accs[(t, n)] = acc
 
-        def add_bias(t):
-            logits = soft_pool.tile([P, A], F32)
-            for n in range(HALVES):
-                cols = slice(n * BANK, (n + 1) * BANK)
-                nc.vector.tensor_tensor(out=logits[:, cols], in0=accs[(t, n)][:], in1=bias_bc[:, cols], op=ALU.add)
-            logit_tiles[t] = logits
+        def add_bias_half(t, n):
+            if n == 0:
+                logits = soft_pool.tile([P, A], F32)
+                logit_tiles[t] = logits
+            cols = slice(n * BANK, (n + 1) * BANK)
+            nc.vector.tensor_tensor(
+                out=logit_tiles[t][:, cols], in0=accs[(t, n)][:], in1=bias_bc[:, cols], op=ALU.add
+            )
 
-        def row_max(t):
-            neg_max = small.tile([P, HEADS], F32)
+        def row_max_heads(t, first, count):
+            if first == 0:
+                neg_max = small.tile([P, HEADS], F32)
+                neg_maxes[t] = neg_max
+            cols = slice(first * HEAD_COLS, (first + count) * HEAD_COLS)
             nc.vector.tensor_reduce(
-                out=neg_max[:],
-                in_=logit_tiles[t][:].rearrange("p (h d) -> p h d", h=HEADS),
+                out=neg_maxes[t][:, first : first + count],
+                in_=logit_tiles[t][:, cols].rearrange("p (h d) -> p h d", h=count),
                 axis=AXIS.X,
                 op=ALU.max,
                 negate=True,
             )
-            neg_maxes[t] = neg_max
+
+        def add_bias(t):
+            add_bias_half(t, 0)
+            if t < TILES - 1:
+                add_bias_half(t, 1)
+
+        def row_max(t):
+            if t < TILES - 1:
+                row_max_heads(t, 0, HEADS)
+            else:
+                row_max_heads(t, 0, HALF_HEADS)
+                add_bias_half(t, 1)
+                row_max_heads(t, HALF_HEADS, HALF_HEADS)
 
         def exponentials(t):
             expo = soft_pool.tile([P, A], F32)
@@ -279,17 +303,24 @@ def tile_efficientcrossattention_pa_kernel(tc, x, ln_w, ln_b, q_w, q_b, out):
 
         def invert_sums(t):
             inv_sums = small.tile([P, HEADS], F32)
-            nc.vector.reciprocal(out=inv_sums[:], in_=expo_tiles[t][1][:])
             inverse_sums[t] = inv_sums
+            if t < TILES - 1:
+                nc.vector.reciprocal(out=inv_sums[:], in_=expo_tiles[t][1][:])
+                return
+            for heads in two_halves:
+                nc.vector.reciprocal(out=inv_sums[:, heads], in_=expo_tiles[t][1][:, heads])
+                scale_heads(t, heads)
 
-        def scale_store(t):
-            probs = soft_pool.tile([P, A], F32)
-            for h in range(HEADS):
+        def scale_heads(t, heads):
+            if heads.start == 0:
+                probs = soft_pool.tile([P, A], F32)
+                prob_tiles[t] = probs
+            for h in range(heads.start, heads.stop):
                 head = slice(h * HEAD_COLS, (h + 1) * HEAD_COLS)
                 who = "V" if t >= TILES - SUBTILES else "G" if h < 3 else "S"
                 if who == "S":
                     nc.scalar.activation(
-                        out=probs[:, head],
+                        out=prob_tiles[t][:, head],
                         in_=expo_tiles[t][0][:, head],
                         func=ACT.Copy,
                         scale=inverse_sums[t][:, h : h + 1],
@@ -297,14 +328,22 @@ def tile_efficientcrossattention_pa_kernel(tc, x, ln_w, ln_b, q_w, q_b, out):
                 else:
                     engine = nc.vector if who == "V" else nc.gpsimd
                     engine.tensor_scalar(
-                        out=probs[:, head],
+                        out=prob_tiles[t][:, head],
                         in0=expo_tiles[t][0][:, head],
                         scalar1=inverse_sums[t][:, h : h + 1],
                         scalar2=1.0,
                         op0=ALU.mult,
                         op1=ALU.mult,
                     )
-            nc.sync.dma_start(out=out_blocks[t // SUBTILES][:, t % SUBTILES, :], in_=probs[:])
+            cols = slice(heads.start * HEAD_COLS, heads.stop * HEAD_COLS)
+            nc.sync.dma_start(out=out_blocks[t // SUBTILES][:, t % SUBTILES, cols], in_=prob_tiles[t][:, cols])
+
+        def scale_store(t):
+            if t < TILES - LAST_STORES:
+                scale_heads(t, slice(0, HEADS))
+            elif t < TILES - 1:
+                for heads in two_halves:
+                    scale_heads(t, heads)
 
         def run(stage, index):
             if 0 <= index < TILES:
@@ -318,6 +357,10 @@ def tile_efficientcrossattention_pa_kernel(tc, x, ln_w, ln_b, q_w, q_b, out):
                 nc.scalar.copy(out=bias_bc[:, cols], in_=bias_bank[:])
 
         regroup_weights(nc.scalar.copy, 0)
+        nc.scalar.copy(
+            out=affine[:].rearrange("p (s c) -> p s c", s=2),
+            in_=affine_bf[:, :, 0].rearrange("p s g j -> p s (g j)"),
+        )
         for step in range(-LEAD_STATS, TILES + LAG_SCALE):
             if step == -4:
                 quantise_weights(0)
@@ -329,13 +372,13 @@ def tile_efficientcrossattention_pa_kernel(tc, x, ln_w, ln_b, q_w, q_b, out):
                 copy_bias()
             run(quantise, step + LEAD_QUANTISE)
             run(invert_sums, step - LAG_SCALE)
-            run(add_bias, step + LEAD_BIAS)
             run(aggregate, step + LEAD_MOMENTS)
             run(row_max, step)
             run(partial_stats, step + LEAD_STATS)
-            run(finish_moments, step + LEAD_MOMENTS)
             run(transpose_affine, step + LEAD_TRANSPOSE)
             run(matmuls, step + LEAD_MATMUL)
+            run(add_bias, step + LEAD_BIAS)
+            run(finish_moments, step + LEAD_MOMENTS)
             run(exponentials, step - LAG_EXP)
             run(regroup, step + LEAD_TRANSPOSE)
             run(centre, step + LEAD_CENTRE)

from contextlib import ExitStack

import concourse.mybir as mybir
from concourse.masks import make_identity

F32 = mybir.dt.float32
BF16 = mybir.dt.bfloat16
U32 = mybir.dt.uint32
U8 = mybir.dt.uint8
FP8X4 = mybir.dt.float8_e4m3fn_x4
ALU = mybir.AluOpType
ACT = mybir.ActivationFunctionType
AXIS = mybir.AxisListType

P = 128
TOKENS = 4 * 512
D = 1024
A = 1024
HEADS = 4
HEAD_COLS = A // HEADS
HALF_HEADS = HEADS // 2
LAST_STORES = 3
EPS = 1e-5

PACK = 4
K_PASS = P * PACK
PASSES = D // K_PASS
CHUNKS = D // P
TILES = TOKENS // P
SUBTILES = 2
BLOCK = P * SUBTILES
BLOCKS = TOKENS // BLOCK
BANK = 512
HALVES = A // BANK
STAT_COLS = 512
STAT_DIM = 6

assert SUBTILES == PASSES
LEAD_STATS = 10
LEAD_MOMENTS = 9
LEAD_CENTRE = 8
LEAD_TRANSPOSE = 5
LEAD_QUANTISE = 3
LEAD_MATMUL = 1
LEAD_BIAS = 1
LAG_EXP = 1
LAG_SCALE = 2

FLOPS = 2 * TOKENS * D * A


def tile_efficientcrossattention_pa_kernel(tc, x, ln_w, ln_b, q_w, q_b, out):
    nc = tc.nc
    x_blocks = x.flatten_outer_dims().rearrange("(b p i) k -> b p i k", p=P, i=SUBTILES)
    out_blocks = out.flatten_outer_dims().rearrange("(b p i) a -> b p i a", p=P, i=SUBTILES)

    with ExitStack() as ctx:
        const = ctx.enter_context(tc.tile_pool(name="const", bufs=1))
        x_pool = ctx.enter_context(tc.tile_pool(name="x", bufs=BLOCKS))
        hat_pool = ctx.enter_context(tc.tile_pool(name="hat", bufs=8))
        norm_pool = ctx.enter_context(tc.tile_pool(name="norm", bufs=6))
        code_pool = ctx.enter_context(tc.tile_pool(name="code", bufs=6))
        small = ctx.enter_context(tc.tile_pool(name="small", bufs=16))
        soft_pool = ctx.enter_context(tc.tile_pool(name="soft", bufs=5))
        psum_t = ctx.enter_context(tc.psum_pool(name="psum_t", bufs=4))
        psum_q = ctx.enter_context(tc.psum_pool(name="psum_q", bufs=4))
        ctx.enter_context(tc.manual_schedule())

        affine_bf = const.tile([P, 2, 2, PASSES, PACK], BF16)
        bias_row = const.tile([P, A], BF16)
        nc.gpsimd.memset(bias_row[:], 0.0)
        x_tiles = []
        for b in range(BLOCKS):
            x_blk = x_pool.tile([P, SUBTILES, D], BF16)
            x_tiles.append(x_blk)
        w_raw = const.tile([P, PASSES, PACK, A], BF16)
        w_view = q_w.rearrange("(g p j) n -> g p j n", j=PACK, p=P)

        def load_x(b):
            nc.sync.dma_start(out=x_tiles[b][:], in_=x_blocks[b])

        def load_tile(t):
            b, i = t // SUBTILES, t % SUBTILES
            nc.sync.dma_start(out=x_tiles[b][:, i, :], in_=x_blocks[b][:, i, :])

        def load_w(g):
            nc.sync.dma_start(out=w_raw[:, g], in_=w_view[g])

        load_tile(0)
        load_tile(1)
        load_x(1)
        load_w(0)
        load_x(2)
        for s, vec in enumerate((ln_w, ln_b)):
            nc.sync.dma_start(out=affine_bf[:, s, 0], in_=vec.rearrange("(g p j) -> p g j", p=P, j=PACK))
        nc.sync.dma_start(out=bias_row[0:1, :], in_=q_b.unsqueeze(0))
        load_w(1)
        for b in range(3, BLOCKS):
            load_x(b)

        ident = const.tile([P, P], F32)
        make_identity(nc, ident[:])
        neg_half = const.tile([P, SUBTILES], F32)
        nc.vector.memset(neg_half[:], -0.5)
        warm = const.tile([P, 1], F32)
        nc.scalar.activation(out=warm[:], in_=neg_half[:, 0:1], func=ACT.Exp)
        affine = const.tile([P, 2 * CHUNKS], F32)

        ones = const.tile([P, P], BF16)
        nc.gpsimd.memset(ones[:], 1.0)
        bias_bc = const.tile([P, A], BF16)

        w_grouped = const.tile([P, PASSES, A, PACK], BF16, align_bytes=64)
        w_codes = const.tile([P, PASSES, A], U32, align_bytes=64)
        w_scales = const.tile([P, PASSES, A], U8, align_bytes=64)

        def regroup_weights(copy, g):
            for n in range(HALVES):
                cols = slice(n * BANK, (n + 1) * BANK)
                copy(
                    out=w_grouped[:, g, cols, :].rearrange("p (c i) j -> p c j i", i=4),
                    in_=w_raw[:, g, :, cols].rearrange("p j (c i) -> p c j i", i=4),
                )

        def quantise_weights(g):
            for n in range(HALVES):
                cols = slice(n * BANK, (n + 1) * BANK)
                nc.vector.quantize_mx(
                    out=w_codes[:, g, cols].bitcast(FP8X4),
                    scales=w_scales[:, g, cols],
                    in_=w_grouped[:, g, cols, :].rearrange("p n j -> p (n j)"),
                )

        stat_tiles = {}
        mean_vars = {}
        moments = {}
        x_hats = {}
        plane_tiles = {}
        grouped_tiles = {}
        operands = {}
        accs = {}
        logit_tiles = {}
        neg_maxes = {}
        expo_tiles = {}
        inverse_sums = {}
        two_halves = [slice(0, HALF_HEADS), slice(HALF_HEADS, HEADS)]
        prob_tiles = {}

        def partial_stats(t):
            stat = small.tile([P, (D // STAT_COLS) * STAT_DIM], F32)
            for h in range(D // STAT_COLS):
                nc.vector.bn_stats(
                    out=stat[:, h * STAT_DIM : (h + 1) * STAT_DIM],
                    in_=x_tiles[t // SUBTILES][:, t % SUBTILES, h * STAT_COLS : (h + 1) * STAT_COLS],
                )
            stat_tiles[t] = stat

        def aggregate(t):
            if t % SUBTILES == 0:
                mean_var = small.tile([P, SUBTILES, 2], F32)
                mean_vars[t // SUBTILES] = mean_var
            nc.vector.bn_aggr(out=mean_vars[t // SUBTILES][:, t % SUBTILES, :], in_=stat_tiles[t][:])

        def finish_moments(t):
            if t % SUBTILES == SUBTILES - 1:
                mean_var = mean_vars[t // SUBTILES]
                neg_mean = small.tile([P, SUBTILES], F32)
                var_eps = small.tile([P, SUBTILES], F32)
                nc.gpsimd.tensor_scalar(
                    out=neg_mean[:], in0=mean_var[:, :, 0], scalar1=-1.0, scalar2=0.0, op0=ALU.mult, op1=ALU.add
                )
                nc.gpsimd.tensor_scalar(
                    out=var_eps[:], in0=mean_var[:, :, 1], scalar1=EPS, scalar2=1.0, op0=ALU.add, op1=ALU.mult
                )
                rstd = small.tile([P, SUBTILES], F32)
                nc.gpsimd.tensor_tensor(out=rstd[:], in0=var_eps[:], in1=neg_half[:], op=ALU.pow)
                moments[t // SUBTILES] = (neg_mean, rstd)

        def centre(t):
            neg_mean, rstd = moments[t // SUBTILES]
            i = t % SUBTILES
            x_hat = hat_pool.tile([P, D], F32)
            engine = nc.gpsimd if t >= SUBTILES and t % 2 == 0 else nc.vector
            engine.tensor_scalar(
                out=x_hat[:].rearrange("q (g j p) -> q g j p", g=PASSES, j=PACK),
                in0=x_tiles[t // SUBTILES][:, i, :].rearrange("q (g p j) -> q g j p", g=PASSES, j=PACK),
                scalar1=neg_mean[:, i : i + 1],
                scalar2=rstd[:, i : i + 1],
                op0=ALU.add,
                op1=ALU.mult,
            )
            x_hats[t] = x_hat

        def transpose_affine(v):
            b, g = v // PASSES, v % PASSES
            planes = norm_pool.tile([P, PACK, BLOCK], BF16)
            for j in range(PACK):
                c = g * PACK + j
                bank = psum_t.tile([P, BANK], F32, tag="bank")
                for i in range(SUBTILES):
                    nc.tensor.transpose(
                        bank[:, i * P : (i + 1) * P], x_hats[b * SUBTILES + i][:, c * P : (c + 1) * P], ident[:]
                    )
                nc.scalar.activation(
                    out=planes[:, j, :],
                    in_=bank[:, 0:BLOCK],
                    func=ACT.Identity,
                    scale=affine[:, c : c + 1],
                    bias=affine[:, CHUNKS + c : CHUNKS + c + 1],
                )
            plane_tiles[v] = planes

        def regroup(v):
            b, g = v // PASSES, v % PASSES
            if g == 0:
                grouped = norm_pool.tile([P, PASSES, BLOCK, PACK], BF16, align_bytes=64)
                grouped_tiles[b] = grouped
            nc.scalar.copy(
                out=grouped_tiles[b][:, g].rearrange("p (c i) j -> p c j i", i=4),
                in_=plane_tiles[v][:].rearrange("p j (c i) -> p c j i", i=4),
            )

        def quantise(v):
            if v % PASSES == PASSES - 1:
                b = v // PASSES
                x_codes = code_pool.tile([P, PASSES, BLOCK], U32, align_bytes=64)
                x_scales = code_pool.tile([P, PASSES, BLOCK], U8, align_bytes=64)
                nc.vector.quantize_mx(
                    out=x_codes[:].rearrange("p g t -> p (g t)").bitcast(FP8X4),
                    scales=x_scales[:].rearrange("p g t -> p (g t)"),
                    in_=grouped_tiles[b][:].rearrange("p g t j -> p (g t j)"),
                )
                operands[b] = (x_codes, x_scales)

        def matmuls(t):
            b, i = t // SUBTILES, t % SUBTILES
            tok = slice(i * P, (i + 1) * P)
            for n in range(HALVES):
                cols = slice(n * BANK, (n + 1) * BANK)
                acc = psum_q.tile([P, BANK], F32, tag="acc")
                for g in range(PASSES):
                    x_codes, x_scales = operands[b]
                    nc.tensor.matmul_mx(
                        out=acc[:],
                        lhsT=x_codes[:, g, tok].bitcast(FP8X4),
                        lhsT_scale=x_scales[:, g, tok],
                        rhs=w_codes[:, g, cols].bitcast(FP8X4),
                        rhs_scale=w_scales[:, g, cols],
                        start=(g == 0),
                        stop=(g == PASSES - 1),
                    )
                accs[(t, n)] = acc

        def add_bias_half(t, n):
            if n == 0:
                logits = soft_pool.tile([P, A], F32)
                logit_tiles[t] = logits
            cols = slice(n * BANK, (n + 1) * BANK)
            nc.vector.tensor_tensor(
                out=logit_tiles[t][:, cols], in0=accs[(t, n)][:], in1=bias_bc[:, cols], op=ALU.add
            )

        def row_max_heads(t, first, count):
            if first == 0:
                neg_max = small.tile([P, HEADS], F32)
                neg_maxes[t] = neg_max
            cols = slice(first * HEAD_COLS, (first + count) * HEAD_COLS)
            nc.vector.tensor_reduce(
                out=neg_maxes[t][:, first : first + count],
                in_=logit_tiles[t][:, cols].rearrange("p (h d) -> p h d", h=count),
                axis=AXIS.X,
                op=ALU.max,
                negate=True,
            )

        def add_bias(t):
            add_bias_half(t, 0)
            if t < TILES - 1:
                add_bias_half(t, 1)

        def row_max(t):
            if t < TILES - 1:
                row_max_heads(t, 0, HEADS)
            else:
                row_max_heads(t, 0, HALF_HEADS)
                add_bias_half(t, 1)
                row_max_heads(t, HALF_HEADS, HALF_HEADS)

        def exponentials(t):
            expo = soft_pool.tile([P, A], F32)
            sums = small.tile([P, HEADS], F32)
            for h in range(HEADS):
                head = slice(h * HEAD_COLS, (h + 1) * HEAD_COLS)
                nc.scalar.activation(
                    out=expo[:, head],
                    in_=logit_tiles[t][:, head],
                    func=ACT.Exp,
                    bias=neg_maxes[t][:, h : h + 1],
                    scale=1.0,
                    accum_out=sums[:, h : h + 1],
                )
            expo_tiles[t] = (expo, sums)

        def invert_sums(t):
            inv_sums = small.tile([P, HEADS], F32)
            inverse_sums[t] = inv_sums
            if t < TILES - 1:
                nc.vector.reciprocal(out=inv_sums[:], in_=expo_tiles[t][1][:])
                return
            for heads in two_halves:
                nc.vector.reciprocal(out=inv_sums[:, heads], in_=expo_tiles[t][1][:, heads])
                scale_heads(t, heads)

        def scale_heads(t, heads):
            if heads.start == 0:
                probs = soft_pool.tile([P, A], F32)
                prob_tiles[t] = probs
            for h in range(heads.start, heads.stop):
                head = slice(h * HEAD_COLS, (h + 1) * HEAD_COLS)
                who = "V" if t >= TILES - SUBTILES else "G" if h < 3 else "S"
                if who == "S":
                    nc.scalar.activation(
                        out=prob_tiles[t][:, head],
                        in_=expo_tiles[t][0][:, head],
                        func=ACT.Copy,
                        scale=inverse_sums[t][:, h : h + 1],
                    )
                else:
                    engine = nc.vector if who == "V" else nc.gpsimd
                    engine.tensor_scalar(
                        out=prob_tiles[t][:, head],
                        in0=expo_tiles[t][0][:, head],
                        scalar1=inverse_sums[t][:, h : h + 1],
                        scalar2=1.0,
                        op0=ALU.mult,
                        op1=ALU.mult,
                    )
            cols = slice(heads.start * HEAD_COLS, heads.stop * HEAD_COLS)
            nc.sync.dma_start(out=out_blocks[t // SUBTILES][:, t % SUBTILES, cols], in_=prob_tiles[t][:, cols])

        def scale_store(t):
            if t < TILES - LAST_STORES:
                scale_heads(t, slice(0, HEADS))
            elif t < TILES - 1:
                for heads in two_halves:
                    scale_heads(t, heads)

        def run(stage, index):
            if 0 <= index < TILES:
                stage(index)

        def copy_bias():
            for n in range(HALVES):
                cols = slice(n * BANK, (n + 1) * BANK)
                bias_bank = psum_q.tile([P, BANK], F32, tag="acc")
                nc.tensor.matmul(bias_bank[:], lhsT=ones[:], rhs=bias_row[:, cols], start=True, stop=True)
                nc.scalar.copy(out=bias_bc[:, cols], in_=bias_bank[:])

        regroup_weights(nc.scalar.copy, 0)
        nc.scalar.copy(
            out=affine[:].rearrange("p (s c) -> p s c", s=2),
            in_=affine_bf[:, :, 0].rearrange("p s g j -> p s (g j)"),
        )
        for step in range(-LEAD_STATS, TILES + LAG_SCALE):
            if step == -4:
                quantise_weights(0)
            if step == -4:
                regroup_weights(nc.vector.tensor_copy, 1)
            if step == -2:
                quantise_weights(1)
            if step == -3:
                copy_bias()
            run(quantise, step + LEAD_QUANTISE)
            run(invert_sums, step - LAG_SCALE)
            run(aggregate, step + LEAD_MOMENTS)
            run(row_max, step)
            run(partial_stats, step + LEAD_STATS)
            run(transpose_affine, step + LEAD_TRANSPOSE)
            run(matmuls, step + LEAD_MATMUL)
            run(add_bias, step + LEAD_BIAS)
            run(finish_moments, step + LEAD_MOMENTS)
            run(exponentials, step - LAG_EXP)
            run(regroup, step + LEAD_TRANSPOSE)
            run(centre, step + LEAD_CENTRE)
            run(scale_store, step - LAG_SCALE)
